import numpy as np
import ml_dtypes


def mxq(x, axis, fmt="e4m3"):
    dtype, down = {"e4m3": (ml_dtypes.float8_e4m3fn, 7), "e5m2": (ml_dtypes.float8_e5m2, 14)}[fmt]
    v = np.moveaxis(np.asarray(x, np.float32).astype(ml_dtypes.bfloat16).astype(np.float64), axis, -1)
    blocks = v.reshape(v.shape[:-1] + (-1, 32))
    amax = np.abs(blocks).max(-1, keepdims=True)
    byte = np.maximum(np.where(amax > 0, np.frexp(amax)[1] - 1 + 127, 0) - down, 1)
    scale = np.exp2(byte - 127.0)
    codes = (blocks / scale).astype(np.float32).astype(dtype).astype(np.float64)
    return np.moveaxis((codes * scale).reshape(v.shape), -1, axis)


WIDE = False


def mx_kscale(k):
    if not WIDE:
        return np.ones(k)
    levels = np.array([10, -10, 5, -5, 0])
    if k % 512:
        return np.exp2(np.random.permutation(np.resize(levels, k // 32))).repeat(32)
    a = np.empty((k // 512, 16))
    for p in range(k // 512):
        a[p, :8] = np.random.permutation(np.resize(levels, 8))
        for g in range(8):
            far = levels[np.abs(levels - a[p, g]) >= 10]
            a[p, g + 8] = far[np.random.randint(len(far))]
    return np.exp2(a.ravel()).repeat(32)


BF16 = ml_dtypes.bfloat16


def bf(x):
    return np.asarray(x, np.float32).astype(BF16)


def f64(x):
    return np.asarray(x).astype(np.float64)


B, S, D, H = 1, 256, 2048, 16
HD = D // H
HALF = HD // 2
ROPE_BASE = 10000.0


def apply_rope(x, cos, sin):
    x1, x2 = np.split(x, 2, axis=-1)
    c = cos[None, None]
    s = sin[None, None]
    return np.concatenate([x1 * c - x2 * s, x1 * s + x2 * c], axis=-1)


def draw0():
    s = mx_kscale(D)
    inv_freq = 1.0 / (ROPE_BASE ** (f64(np.arange(HALF)) / HALF))
    pos = f64(np.random.randint(0, S) + np.arange(S))
    ang = pos[:, None] * inv_freq[None, :]
    return {"x": bf(np.random.standard_normal((B, S, D)) * s),
            "w_qkv": bf(np.random.standard_normal((D, 3 * D)) / np.sqrt(D) / s[:, None]),
            "b_qkv": bf(np.random.standard_normal(3 * D) * 0.5),
            "rope_cos": bf(np.cos(ang)),
            "rope_sin": bf(np.sin(ang))}


def core(x, w_qkv, b_qkv, rope_cos, rope_sin):
    cos, sin = f64(rope_cos), f64(rope_sin)
    qkv = (mxq(f64(x), 2, "e4m3") @ mxq(f64(w_qkv), 0, "e4m3")) + f64(b_qkv)
    qkv = qkv.reshape(B, S, 3, H, HD)
    qkv = np.transpose(qkv, (2, 0, 3, 1, 4))
    q, k, v = qkv[0], qkv[1], qkv[2]
    return apply_rope(q, cos, sin), apply_rope(k, cos, sin), np.ascontiguousarray(v)


def e4m3fn_bytes(y):
    return np.clip(np.asarray(y, np.float64), -448.0, 448.0).astype(np.float32).astype(ml_dtypes.float8_e4m3fn).view(np.uint8)


def e4m3fn_values(b):
    return np.asarray(b, np.uint8).view(ml_dtypes.float8_e4m3fn).astype(np.float64)


def setup_inputs():
    d = draw0()
    x0 = np.asarray(d['w_qkv']).astype(np.float64)
    s = (np.max(np.abs(x0), axis=(1,), keepdims=True) / 448.0).astype(np.float32)
    out = {}
    for k, v in d.items():
        if k == 'w_qkv':
            out['w_qkv_bytes'] = e4m3fn_bytes(x0 / s.astype(np.float64))
            out['w_qkv_scale'] = s
        else:
            out[k] = v
    return out


def reference(x, w_qkv_bytes, w_qkv_scale, b_qkv, rope_cos, rope_sin):
    return core(x, e4m3fn_values(w_qkv_bytes) * w_qkv_scale.astype(np.float64), b_qkv, rope_cos, rope_sin)

@@ -1,0 +1,358 @@
+from contextlib import ExitStack
+
+import concourse.masks as masks
+import concourse.mybir as mybir
+
+F32 = mybir.dt.float32
+BF16 = mybir.dt.bfloat16
+U32 = mybir.dt.uint32
+U8 = mybir.dt.uint8
+FP8 = mybir.dt.float8_e4m3fn
+FP8X4 = mybir.dt.float8_e4m3fn_x4
+ACT = mybir.ActivationFunctionType
+ALU = mybir.AluOpType
+
+P = 128
+S_LEN = 256
+D = 2048
+HD = 128
+N_OUT = 3 * D
+PASSES = 4
+NC = 512
+CHUNKS = N_OUT // NC
+ROT_CHUNKS = 2 * D // NC
+UNITS = CHUNKS * PASSES
+PAIRS = 2 * ROT_CHUNKS
+AHEAD = 16
+LEAD = 4
+LAG = 5
+PEW = 96
+SPLIT = 2
+V_HEAD2 = 4
+V_HEAD1 = 8
+V_TAKE = (0, 1, 2)
+V_STOP = 40
+
+FLOPS = 2 * S_LEN * D * N_OUT
+
+
+def v_planes(i):
+    if i < V_HEAD2:
+        return 2
+    if i < V_HEAD1:
+        return 1
+    return 1 if (i % 4 in V_TAKE and i < V_STOP) else 0
+
+
+def s_cols(i):
+    return 0
+
+
+def tile_multiheadattentionusingsdp_pa_kernel(
+    tc, x, w_qkv_bytes, w_qkv_scale, b_qkv, rope_cos, rope_sin, out_0, out_1, out_2
+):
+    nc = tc.nc
+    outs = (out_0, out_1, out_2)
+    w_view = w_qkv_bytes.rearrange("(g p t) n -> g p t n", g=PASSES, p=P, t=4)
+
+    with ExitStack() as ctx:
+        const = ctx.enter_context(tc.tile_pool(name="const", bufs=1))
+        wbp = ctx.enter_context(tc.tile_pool(name="wbp", bufs=AHEAD + 8))
+        widep = ctx.enter_context(tc.tile_pool(name="widep", bufs=LEAD + 3))
+        grpp = ctx.enter_context(tc.tile_pool(name="grpp", bufs=5))
+        codep = ctx.enter_context(tc.tile_pool(name="codep", bufs=3))
+        rotp = ctx.enter_context(tc.tile_pool(name="rotp", bufs=3))
+        stp = ctx.enter_context(tc.tile_pool(name="stp", bufs=6))
+        psa = ctx.enter_context(tc.psum_pool(name="psa", bufs=3))
+        pso = ctx.enter_context(tc.psum_pool(name="pso", bufs=2))
+        psi = ctx.enter_context(tc.psum_pool(name="psi", bufs=3))
+        ctx.enter_context(tc.manual_schedule())
+
+        wb = {}
+        wide = {}
+        grp = {}
+        pint = {}
+        wc = {}
+        ws = {}
+        acc = {}
+        rot = {}
+        o2 = {}
+
+        def load(i):
+            j, g = divmod(i, PASSES)
+            wb[i] = wbp.tile([P, 4, NC], U8, name="wb", tag="wb")
+            src = w_view[g][:, :, j * NC : (j + 1) * NC]
+            if i < SPLIT:
+                for t in range(4):
+                    nc.sync.dma_start(out=wb[i][:, t, :], in_=src[:, t, :])
+            else:
+                nc.sync.dma_start(out=wb[i][:], in_=src)
+
+        warm = const.tile([P, 2], F32, name="warm")
+        nc.vector.memset(warm[:], 0.0)
+        nc.scalar.activation(out=warm[:, 1:2], in_=warm[:, 0:1], func=ACT.Copy)
+        sgn = const.tile([P, 1], F32, name="sgn")
+        nc.vector.memset(sgn[0:64, :], 1.0)
+        nc.vector.memset(sgn[64:128, :], -1.0)
+        ident = const.tile([P, P], F32, name="ident")
+        masks.make_identity(nc, ident[:])
+        braw = const.tile([P, P], BF16, name="braw")
+        nc.gpsimd.memset(braw[:], 0.0)
+        identb = const.tile([P, P], BF16, name="identb")
+        nc.vector.tensor_copy(out=identb[:], in_=ident[:])
+
+        sc = const.tile([P, PASSES, 4], F32, name="sc")
+        nc.sync.dma_start(
+            out=sc[:], in_=w_qkv_scale.rearrange("(g p t) o -> p g (t o)", g=PASSES, p=P, t=4)
+        )
+        for i in range(5):
+            load(i)
+        craw = const.tile([P, 2, 2, 64], BF16, name="craw")
+        nc.sync.dma_start(out=craw[:, 0], in_=rope_cos.rearrange("(m p) d -> p m d", p=P))
+        nc.sync.dma_start(out=craw[:, 1], in_=rope_sin.rearrange("(m p) d -> p m d", p=P))
+        nc.sync.dma_start(out=braw[0:32, :], in_=b_qkv[0 : 2 * D].rearrange("(c d) -> c d", d=HD))
+        x_sb = const.tile([P, 2, D], BF16, name="x_sb")
+        x_view = x.rearrange("o (m p) k -> p (o m) k", p=P)
+        nc.sync.dma_start(out=x_sb[:, 0, :], in_=x_view[:, 0, :])
+        load(5)
+        nc.sync.dma_start(out=x_sb[:, 1, :], in_=x_view[:, 1, :])
+        for i in range(6, AHEAD - LEAD):
+            load(i)
+        bv = const.tile([P, D], BF16, name="bv")
+
+        perm = const.tile([P, P], F32, name="perm")
+        zt = const.tile([P, 2, 2, P], F32, name="zt")
+        bf32 = const.tile([P, P], F32, name="bf32")
+        cs = const.tile([P, 2, S_LEN], F32, name="cs")
+        bias = const.tile([P, 32], F32, name="bias")
+        xg = const.tile([P, PASSES, S_LEN, 4], BF16, name="xg", align_bytes=64)
+        xc = const.tile([P, PASSES, S_LEN], U32, name="xc", align_bytes=64)
+        xs = const.tile([P, PASSES, S_LEN], U8, name="xs", align_bytes=64)
+        xt = {}
+        small = {}
+
+        def x_transposes(g):
+            xt[g] = psa.tile([P, 2, S_LEN], F32, name="xt", tag="acc")
+            for m in range(2):
+                words = x_sb[:, m, :].bitcast(F32)
+                for u in range(2):
+                    nc.tensor.transpose(
+                        xt[g][:, u, m * P : (m + 1) * P],
+                        words[:, 256 * g + u : 256 * (g + 1) : 2],
+                        ident[:],
+                    )
+
+        def small_prep():
+            nc.vector.tensor_copy(out=perm[:, 0:64], in_=ident[:, 64:128])
+            nc.vector.tensor_copy(out=perm[:, 64:128], in_=ident[:, 0:64])
+            nc.vector.tensor_copy(out=zt[:, :, :, 0:64], in_=craw[:])
+            nc.vector.tensor_copy(out=zt[:, :, :, 64:128], in_=craw[:])
+            nc.vector.tensor_copy(out=bf32[:], in_=braw[:])
+            small["pcs"] = pso.tile([P, 2, S_LEN], F32, name="pcs", tag="o2")
+            for c in range(2):
+                for m in range(2):
+                    nc.tensor.transpose(
+                        small["pcs"][:, c, m * P : (m + 1) * P], zt[:, c, m, :], ident[:]
+                    )
+            small["pb"] = pso.tile([P, P], F32, name="pb", tag="o2")
+            nc.tensor.transpose(small["pb"][:], bf32[:], ident[:])
+
+        def small_out():
+            nc.scalar.copy(out=cs[:, 0, :], in_=small["pcs"][:, 0, :])
+            nc.scalar.activation(
+                out=cs[:, 1, :], in_=small["pcs"][:, 1, :], func=ACT.Copy, scale=sgn[:, 0:1]
+            )
+            nc.scalar.copy(out=bias[:], in_=small["pb"][:, 0:32])
+
+        def xcopy(g):
+            nc.scalar.copy(out=xg[:, g].bitcast(F32), in_=xt[g][:].rearrange("p u r -> p r u"))
+
+        def xquant(g):
+            nc.vector.quantize_mx(
+                out=xc[:, g, :].bitcast(FP8X4),
+                scales=xs[:, g, :],
+                in_=xg[:, g].rearrange("p r j -> p (r j)"),
+            )
+
+        def plane(i, t):
+            g = i % PASSES
+            if t == 0:
+                wide[i] = widep.tile([P, 4, NC], BF16, name="wide", tag="wide")
+            src = wb[i][:, t, :].bitcast(FP8)
+            if t >= 4 - v_planes(i):
+                nc.vector.tensor_scalar(
+                    out=wide[i][:, t, :], in0=src, scalar1=sc[:, g, t : t + 1],
+                    scalar2=None, op0=ALU.mult,
+                )
+            else:
+                nc.scalar.activation(
+                    out=wide[i][:, t, :], in_=src, func=ACT.Copy, scale=sc[:, g, t : t + 1]
+                )
+
+        def pe_inter(i):
+            pint[i] = psi.tile([P, PEW, 4], BF16, name="pint", tag="pint")
+            nc.tensor.matmul(
+                out=pint[i][:].rearrange("p n t -> p (n t)"),
+                lhsT=identb[:],
+                rhs=wide[i][:, :, 0:PEW].rearrange("p t n -> p n t"),
+                start=True, stop=True,
+            )
+
+        def pe_evac(i):
+            grp[i] = grpp.tile([P, NC, 4], BF16, name="grp", tag="grp", align_bytes=64)
+            nc.scalar.copy(out=grp[i][:, 0:PEW, :], in_=pint[i][:])
+            sw = s_cols(i)
+            if sw:
+                nc.scalar.copy(
+                    out=grp[i][:, PEW : PEW + sw, :],
+                    in_=wide[i][:, :, PEW : PEW + sw].rearrange("p t n -> p n t"),
+                )
+
+        def inter(i):
+            c0 = PEW + s_cols(i)
+            nc.vector.tensor_copy(
+                out=grp[i][:, c0:NC, :].rearrange("p (c q) t -> p c t q", q=4),
+                in_=wide[i][:, :, c0:NC].rearrange("p t (c q) -> p c t q", q=4),
+            )
+
+        def quant(i):
+            j, g = divmod(i, PASSES)
+            if g == 0:
+                wc[j] = codep.tile([P, PASSES, NC], U32, name="wc", tag="wc", align_bytes=64)
+                ws[j] = codep.tile([P, PASSES, NC], U8, name="ws", tag="ws", align_bytes=64)
+            nc.vector.quantize_mx(
+                out=wc[j][:, g, :].bitcast(FP8X4),
+                scales=ws[j][:, g, :],
+                in_=grp[i][:].rearrange("p n t -> p (n t)"),
+            )
+
+        def mx_rot(q):
+            j, pr = divmod(q, 2)
+            acc[q] = psa.tile([P, 2, S_LEN], F32, name="acc", tag="acc")
+            for e in range(2):
+                cols = slice((2 * pr + e) * HD, (2 * pr + e + 1) * HD)
+                for g in range(PASSES):
+                    nc.tensor.matmul_mx(
+                        out=acc[q][:, e, :],
+                        lhsT=wc[j][:, g, cols].bitcast(FP8X4),
+                        lhsT_scale=ws[j][:, g, cols],
+                        rhs=xc[:, g, :].bitcast(FP8X4),
+                        rhs_scale=xs[:, g, :],
+                        start=(g == 0),
+                        stop=(g == PASSES - 1),
+                    )
+
+        def rope(q):
+            r = rotp.tile([P, 2, 2, S_LEN], F32, name="rot", tag="rot")
+            for e in range(2):
+                c = 2 * q + e
+                nc.vector.scalar_tensor_tensor(
+                    out=r[:, :, e, :],
+                    in0=acc[q][:, e, :].unsqueeze(1).to_broadcast([P, 2, S_LEN]),
+                    scalar=bias[:, c : c + 1],
+                    in1=cs[:], op0=ALU.add, op1=ALU.mult,
+                )
+            o2[q] = pso.tile([P, 2, 2, HD], F32, name="o2", tag="o2")
+            for e in range(2):
+                for m in range(2):
+                    tok = slice(m * P, (m + 1) * P)
+                    nc.tensor.matmul(
+                        out=o2[q][:, m, e, :], lhsT=r[:, 0, e, tok], rhs=ident[:],
+                        is_transpose=True, start=True, stop=False,
+                    )
+                    nc.tensor.matmul(
+                        out=o2[q][:, m, e, :], lhsT=r[:, 1, e, tok], rhs=perm[:],
+                        is_transpose=True, start=False, stop=True,
+                    )
+
+        def evac(q):
+            st = stp.tile([P, 2, 2, HD], F32, name="st", tag="st")
+            nc.scalar.copy(out=st[:], in_=o2[q][:])
+            dst = outs[q // 8]
+            h0 = 2 * (q % 8)
+            for m in range(2):
+                nc.sync.dma_start(
+                    out=dst[0, h0 : h0 + 2, m * P : (m + 1) * P, :].rearrange("h s d -> s h d"),
+                    in_=st[:, m],
+                )
+
+        def mx_v(i):
+            j, g = divmod(i, PASSES)
+            for m in range(2):
+                if g == 0 and j % 2 == 0:
+                    acc[(j, m)] = psa.tile([P, NC], F32, name="accv", tag="acc")
+                elif g == 0:
+                    acc[(j, m)] = pso.tile([P, NC], F32, name="accv", tag="o2")
+                tok = slice(m * P, (m + 1) * P)
+                nc.tensor.matmul_mx(
+                    out=acc[(j, m)][:],
+                    lhsT=xc[:, g, tok].bitcast(FP8X4),
+                    lhsT_scale=xs[:, g, tok],
+                    rhs=wc[j][:, g, :].bitcast(FP8X4),
+                    rhs_scale=ws[j][:, g, :],
+                    start=(g == 0),
+                    stop=(g == PASSES - 1),
+                )
+
+        def v_out(j):
+            for m in range(2):
+                c0 = (j - ROT_CHUNKS) * NC
+                st = stp.tile([P, 4, HD], F32, name="st", tag="st")
+                nc.vector.tensor_tensor(
+                    out=st[:].rearrange("p h d -> p (h d)"), in0=acc[(j, m)][:],
+                    in1=bv[:, c0 : c0 + NC], op=ALU.add,
+                )
+                h0 = c0 // HD
+                nc.sync.dma_start(
+                    out=out_2[0, h0 : h0 + 4, m * P : (m + 1) * P, :].rearrange("h s d -> s h d"),
+                    in_=st[:],
+                )
+
+        def pair_at(step):
+            j, r = divmod(step, PASSES)
+            return 2 * j + r if (r < 2 and 0 <= j < ROT_CHUNKS) else None
+
+        for i in range(-LEAD, UNITS + LAG + 6):
+            j, g = divmod(i, PASSES)
+            if 0 <= i + AHEAD < UNITS:
+                load(i + AHEAD)
+            if i == 8:
+                nc.sync.dma_start(out=bv[:], in_=b_qkv[2 * D : 3 * D].partition_broadcast(P))
+            if i == 2:
+                small_out()
+            if 0 <= i - 2 < PASSES:
+                xcopy(i - 2)
+            for t in range(4):
+                if 0 <= i + LEAD < UNITS:
+                    plane(i + LEAD, t)
+                if t == 1 and 0 <= i + 2 < UNITS:
+                    pe_evac(i + 2)
+                if t == 2 and pair_at(i - LAG - 4) is not None:
+                    evac(pair_at(i - LAG - 4))
+            if 0 <= i + LEAD < UNITS:
+                pe_inter(i + LEAD)
+            if 0 <= i + 1 < UNITS:
+                inter(i + 1)
+            if 0 <= i < UNITS:
+                quant(i)
+            if i == 0:
+                small_prep()
+            if i == 1:
+                for p in range(3):
+                    x_transposes(p)
+            if i == 3:
+                x_transposes(3)
+            if i in (4, 5):
+                xquant(2 * i - 8)
+                xquant(2 * i - 7)
+            if pair_at(i - LAG) is not None:
+                mx_rot(pair_at(i - LAG))
+            if pair_at(i - LAG - 2) is not None:
+                rope(pair_at(i - LAG - 2))
+            if ROT_CHUNKS * PASSES <= i < UNITS:
+                mx_v(i)
+            if g == 0 and ROT_CHUNKS <= j - 1 < CHUNKS - 2:
+                v_out(j - 1)
+            if i == UNITS - 1:
+                v_out(CHUNKS - 2)
+                v_out(CHUNKS - 1)

@@ -211,8 +211,8 @@ def tile_multiheadattentionusingsdp_pa_kernel(
         def inter(i):
             c0 = PEW + s_cols(i)
             nc.vector.tensor_copy(
-                out=grp[i][:, c0:NC, :].rearrange("p (c q) t -> p c t q", q=4),
-                in_=wide[i][:, :, c0:NC].rearrange("p t (c q) -> p c t q", q=4),
+                out=grp[i][:, c0:NC, :].rearrange("p (c q) t -> p c t q", q=8),
+                in_=wide[i][:, :, c0:NC].rearrange("p t (c q) -> p c t q", q=8),
             )
 
         def quant(i):

@@ -32,6 +32,7 @@ V_HEAD2 = 4
 V_HEAD1 = 8
 V_TAKE = (0, 1, 2)
 V_STOP = 40
+V_ALSO = 3
 
 FLOPS = 2 * S_LEN * D * N_OUT
 
@@ -41,7 +42,7 @@ def v_planes(i):
         return 2
     if i < V_HEAD1:
         return 1
-    return 1 if (i % 4 in V_TAKE and i < V_STOP) else 0
+    return 1 if ((i % 4 in V_TAKE or i % 8 == V_ALSO) and i < V_STOP) else 0
 
 
 def s_cols(i):

@@ -33,6 +33,7 @@ V_HEAD1 = 8
 V_TAKE = (0, 1, 2)
 V_STOP = 40
 V_ALSO = 3
+GW = 256
 
 FLOPS = 2 * S_LEN * D * N_OUT
 
@@ -47,6 +48,10 @@ def v_planes(i):
 
 def s_cols(i):
     return 0
+
+
+def g_cols(i):
+    return GW if (i % 4 == 2 and 10 <= i <= 38) else 0
 
 
 def tile_multiheadattentionusingsdp_pa_kernel(
@@ -64,9 +69,10 @@ def tile_multiheadattentionusingsdp_pa_kernel(
         codep = ctx.enter_context(tc.tile_pool(name="codep", bufs=3))
         rotp = ctx.enter_context(tc.tile_pool(name="rotp", bufs=3))
         stp = ctx.enter_context(tc.tile_pool(name="stp", bufs=6))
-        psa = ctx.enter_context(tc.psum_pool(name="psa", bufs=3))
+        trigp = ctx.enter_context(tc.tile_pool(name="trigp", bufs=2))
+        psa = ctx.enter_context(tc.psum_pool(name="psa", bufs=4))
         pso = ctx.enter_context(tc.psum_pool(name="pso", bufs=2))
-        psi = ctx.enter_context(tc.psum_pool(name="psi", bufs=3))
+        psi = ctx.enter_context(tc.psum_pool(name="psi", bufs=2))
         ctx.enter_context(tc.manual_schedule())
 
         wb = {}
@@ -210,10 +216,20 @@ def tile_multiheadattentionusingsdp_pa_kernel(
                 )
 
         def inter(i):
-            c0 = PEW + s_cols(i)
+            c0 = PEW + s_cols(i) + g_cols(i)
             nc.vector.tensor_copy(
                 out=grp[i][:, c0:NC, :].rearrange("p (c q) t -> p c t q", q=8),
                 in_=wide[i][:, :, c0:NC].rearrange("p t (c q) -> p c t q", q=8),
+            )
+
+        def g_inter(i):
+            trig = trigp.tile([P, 1], F32, name="trig", tag="trig")
+            nc.vector.memset(trig[:], 1.0)
+            c0 = PEW + s_cols(i)
+            nc.gpsimd.tensor_scalar(
+                out=grp[i][:, c0 : c0 + g_cols(i), :],
+                in0=wide[i][:, :, c0 : c0 + g_cols(i)].rearrange("p t n -> p n t"),
+                scalar1=trig[:, 0:1], scalar2=0.0, op0=ALU.mult, op1=ALU.add,
             )
 
         def quant(i):
@@ -348,7 +364,10 @@ def tile_multiheadattentionusingsdp_pa_kernel(
                 xquant(2 * i - 7)
             if pair_at(i - LAG) is not None:
                 mx_rot(pair_at(i - LAG))
-            if pair_at(i - LAG - 2) is not None:
+            if 0 <= i + 2 < UNITS and g_cols(i + 2):
+                g_inter(i + 2)
+            if pair_at(i - LAG - 2) is not None and pair_at(i - LAG - 2) % 2 == 1:
+                rope(pair_at(i - LAG - 2) - 1)
                 rope(pair_at(i - LAG - 2))
             if ROT_CHUNKS * PASSES <= i < UNITS:
                 mx_v(i)

@@ -31,9 +31,9 @@ SPLIT = 2
 V_HEAD2 = 4
 V_HEAD1 = 8
 V_TAKE = (0, 1, 2)
-V_STOP = 40
+V_STOP = 42
 V_ALSO = 3
-GW = 256
+GW = 352
 
 FLOPS = 2 * S_LEN * D * N_OUT
 
@@ -43,7 +43,7 @@ def v_planes(i):
         return 2
     if i < V_HEAD1:
         return 1
-    return 1 if ((i % 4 in V_TAKE or i % 8 == V_ALSO) and i < V_STOP) else 0
+    return 1 if ((i % 4 in V_TAKE or i % 4 == V_ALSO) and i < V_STOP) else 0
 
 
 def s_cols(i):
@@ -84,6 +84,7 @@ def tile_multiheadattentionusingsdp_pa_kernel(
         acc = {}
         rot = {}
         o2 = {}
+        trig = {}
 
         def load(i):
             j, g = divmod(i, PASSES)
@@ -217,19 +218,23 @@ def tile_multiheadattentionusingsdp_pa_kernel(
 
         def inter(i):
             c0 = PEW + s_cols(i) + g_cols(i)
+            if c0 == NC:
+                return
             nc.vector.tensor_copy(
                 out=grp[i][:, c0:NC, :].rearrange("p (c q) t -> p c t q", q=8),
                 in_=wide[i][:, :, c0:NC].rearrange("p t (c q) -> p c t q", q=8),
             )
 
+        def g_trig(i):
+            trig[i] = trigp.tile([P, 1], F32, name="trig", tag="trig")
+            nc.vector.memset(trig[i][:], 1.0)
+
         def g_inter(i):
-            trig = trigp.tile([P, 1], F32, name="trig", tag="trig")
-            nc.vector.memset(trig[:], 1.0)
             c0 = PEW + s_cols(i)
             nc.gpsimd.tensor_scalar(
                 out=grp[i][:, c0 : c0 + g_cols(i), :],
                 in0=wide[i][:, :, c0 : c0 + g_cols(i)].rearrange("p t n -> p n t"),
-                scalar1=trig[:, 0:1], scalar2=0.0, op0=ALU.mult, op1=ALU.add,
+                scalar1=trig[i][:, 0:1], scalar2=0.0, op0=ALU.mult, op1=ALU.add,
             )
 
         def quant(i):
@@ -350,6 +355,8 @@ def tile_multiheadattentionusingsdp_pa_kernel(
                 pe_inter(i + LEAD)
             if 0 <= i + 1 < UNITS:
                 inter(i + 1)
+            if 0 <= i + 2 < UNITS and g_cols(i + 2):
+                g_trig(i + 2)
             if 0 <= i < UNITS:
                 quant(i)
             if i == 0:

@@ -51,7 +51,7 @@ def s_cols(i):
 
 
 def g_cols(i):
-    return GW if (i % 4 == 2 and 10 <= i <= 38) else 0
+    return GW if (i % 4 == 2 and 10 <= i <= 42) else 0
 
 
 def tile_multiheadattentionusingsdp_pa_kernel(
@@ -301,7 +301,7 @@ def tile_multiheadattentionusingsdp_pa_kernel(
         def mx_v(i):
             j, g = divmod(i, PASSES)
             for m in range(2):
-                if g == 0 and j % 2 == 0:
+                if g == 0 and j != CHUNKS - 2:
                     acc[(j, m)] = psa.tile([P, NC], F32, name="accv", tag="acc")
                 elif g == 0:
                     acc[(j, m)] = pso.tile([P, NC], F32, name="accv", tag="o2")
@@ -349,8 +349,8 @@ def tile_multiheadattentionusingsdp_pa_kernel(
                     plane(i + LEAD, t)
                 if t == 1 and 0 <= i + 2 < UNITS:
                     pe_evac(i + 2)
-                if t == 2 and pair_at(i - LAG - 4) is not None:
-                    evac(pair_at(i - LAG - 4))
+                if t == 2 and pair_at(i - LAG - 5) is not None:
+                    evac(pair_at(i - LAG - 5))
             if 0 <= i + LEAD < UNITS:
                 pe_inter(i + LEAD)
             if 0 <= i + 1 < UNITS:
@@ -378,8 +378,9 @@ def tile_multiheadattentionusingsdp_pa_kernel(
                 rope(pair_at(i - LAG - 2))
             if ROT_CHUNKS * PASSES <= i < UNITS:
                 mx_v(i)
-            if g == 0 and ROT_CHUNKS <= j - 1 < CHUNKS - 2:
-                v_out(j - 1)
+            if i == (CHUNKS - 2) * PASSES:
+                v_out(CHUNKS - 4)
+                v_out(CHUNKS - 3)
             if i == UNITS - 1:
                 v_out(CHUNKS - 2)
                 v_out(CHUNKS - 1)

@@ -27,8 +27,8 @@ AHEAD = 16
 LEAD = 4
 LAG = 5
 PEW = 96
-SPLIT = 2
-V_HEAD2 = 4
+SPLIT = 1
+V_HEAD2 = 5
 V_HEAD1 = 8
 V_TAKE = (0, 1, 2)
 V_STOP = 42
@@ -91,13 +91,17 @@ def tile_multiheadattentionusingsdp_pa_kernel(
             wb[i] = wbp.tile([P, 4, NC], U8, name="wb", tag="wb")
             src = w_view[g][:, :, j * NC : (j + 1) * NC]
             if i < SPLIT:
-                for t in range(4):
-                    nc.sync.dma_start(out=wb[i][:, t, :], in_=src[:, t, :])
+                for t in (0, 2):
+                    nc.sync.dma_start(out=wb[i][:, t : t + 2, :], in_=src[:, t : t + 2, :])
             else:
                 nc.sync.dma_start(out=wb[i][:], in_=src)
 
         warm = const.tile([P, 2], F32, name="warm")
         nc.vector.memset(warm[:], 0.0)
+        sc = const.tile([P, PASSES, 4], F32, name="sc")
+        nc.scalar.dma_start(
+            out=sc[:], in_=w_qkv_scale.rearrange("(g p t) o -> p g (t o)", g=PASSES, p=P, t=4)
+        )
         nc.scalar.activation(out=warm[:, 1:2], in_=warm[:, 0:1], func=ACT.Copy)
         sgn = const.tile([P, 1], F32, name="sgn")
         nc.vector.memset(sgn[0:64, :], 1.0)
@@ -109,10 +113,6 @@ def tile_multiheadattentionusingsdp_pa_kernel(
         identb = const.tile([P, P], BF16, name="identb")
         nc.vector.tensor_copy(out=identb[:], in_=ident[:])
 
-        sc = const.tile([P, PASSES, 4], F32, name="sc")
-        nc.sync.dma_start(
-            out=sc[:], in_=w_qkv_scale.rearrange("(g p t) o -> p g (t o)", g=PASSES, p=P, t=4)
-        )
         for i in range(5):
             load(i)
         craw = const.tile([P, 2, 2, 64], BF16, name="craw")

@@ -28,7 +28,7 @@ LEAD = 4
 LAG = 5
 PEW = 96
 SPLIT = 1
-V_HEAD2 = 5
+V_HEAD2 = 8
 V_HEAD1 = 8
 V_TAKE = (0, 1, 2)
 V_STOP = 42

@@ -33,7 +33,7 @@ V_HEAD1 = 8
 V_TAKE = (0, 1, 2)
 V_STOP = 42
 V_ALSO = 3
-GW = 352
+GW = 384
 
 FLOPS = 2 * S_LEN * D * N_OUT
 
@@ -232,8 +232,8 @@ def tile_multiheadattentionusingsdp_pa_kernel(
         def g_inter(i):
             c0 = PEW + s_cols(i)
             nc.gpsimd.tensor_scalar(
-                out=grp[i][:, c0 : c0 + g_cols(i), :],
-                in0=wide[i][:, :, c0 : c0 + g_cols(i)].rearrange("p t n -> p n t"),
+                out=grp[i][:, c0 : c0 + g_cols(i), :].rearrange("p (c q) t -> p c t q", q=8),
+                in0=wide[i][:, :, c0 : c0 + g_cols(i)].rearrange("p t (c q) -> p c t q", q=8),
                 scalar1=trig[i][:, 0:1], scalar2=0.0, op0=ALU.mult, op1=ALU.add,
             )
 

@@ -27,13 +27,15 @@ AHEAD = 16
 LEAD = 4
 LAG = 5
 PEW = 96
+PEW_G = 128
 SPLIT = 1
 V_HEAD2 = 8
 V_HEAD1 = 8
 V_TAKE = (0, 1, 2)
-V_STOP = 42
+V_STOP = 44
 V_ALSO = 3
 GW = 384
+S_TAIL = 128
 
 FLOPS = 2 * S_LEN * D * N_OUT
 
@@ -47,11 +49,15 @@ def v_planes(i):
 
 
 def s_cols(i):
-    return 0
+    return S_TAIL if i == UNITS - 1 else 0
 
 
 def g_cols(i):
     return GW if (i % 4 == 2 and 10 <= i <= 42) else 0
+
+
+def pe_cols(i):
+    return PEW_G if g_cols(i) else PEW
 
 
 def tile_multiheadattentionusingsdp_pa_kernel(
@@ -112,6 +118,9 @@ def tile_multiheadattentionusingsdp_pa_kernel(
         nc.gpsimd.memset(braw[:], 0.0)
         identb = const.tile([P, P], BF16, name="identb")
         nc.vector.tensor_copy(out=identb[:], in_=ident[:])
+        perm = const.tile([P, P], F32, name="perm")
+        nc.vector.tensor_copy(out=perm[:, 0:64], in_=ident[:, 64:128])
+        nc.vector.tensor_copy(out=perm[:, 64:128], in_=ident[:, 0:64])
 
         for i in range(5):
             load(i)
@@ -128,7 +137,6 @@ def tile_multiheadattentionusingsdp_pa_kernel(
             load(i)
         bv = const.tile([P, D], BF16, name="bv")
 
-        perm = const.tile([P, P], F32, name="perm")
         zt = const.tile([P, 2, 2, P], F32, name="zt")
         bf32 = const.tile([P, P], F32, name="bf32")
         cs = const.tile([P, 2, S_LEN], F32, name="cs")
@@ -151,8 +159,6 @@ def tile_multiheadattentionusingsdp_pa_kernel(
                     )
 
         def small_prep():
-            nc.vector.tensor_copy(out=perm[:, 0:64], in_=ident[:, 64:128])
-            nc.vector.tensor_copy(out=perm[:, 64:128], in_=ident[:, 0:64])
             nc.vector.tensor_copy(out=zt[:, :, :, 0:64], in_=craw[:])
             nc.vector.tensor_copy(out=zt[:, :, :, 64:128], in_=craw[:])
             nc.vector.tensor_copy(out=bf32[:], in_=braw[:])
@@ -198,17 +204,17 @@ def tile_multiheadattentionusingsdp_pa_kernel(
                 )
 
         def pe_inter(i):
-            pint[i] = psi.tile([P, PEW, 4], BF16, name="pint", tag="pint")
+            pint[i] = psi.tile([P, pe_cols(i), 4], BF16, name="pint", tag="pint")
             nc.tensor.matmul(
                 out=pint[i][:].rearrange("p n t -> p (n t)"),
                 lhsT=identb[:],
-                rhs=wide[i][:, :, 0:PEW].rearrange("p t n -> p n t"),
+                rhs=wide[i][:, :, 0 : pe_cols(i)].rearrange("p t n -> p n t"),
                 start=True, stop=True,
             )
 
         def pe_evac(i):
             grp[i] = grpp.tile([P, NC, 4], BF16, name="grp", tag="grp", align_bytes=64)
-            nc.scalar.copy(out=grp[i][:, 0:PEW, :], in_=pint[i][:])
+            nc.scalar.copy(out=grp[i][:, 0 : pe_cols(i), :], in_=pint[i][:])
             sw = s_cols(i)
             if sw:
                 nc.scalar.copy(
@@ -217,7 +223,7 @@ def tile_multiheadattentionusingsdp_pa_kernel(
                 )
 
         def inter(i):
-            c0 = PEW + s_cols(i) + g_cols(i)
+            c0 = pe_cols(i) + s_cols(i) + g_cols(i)
             if c0 == NC:
                 return
             nc.vector.tensor_copy(
@@ -230,7 +236,7 @@ def tile_multiheadattentionusingsdp_pa_kernel(
             nc.vector.memset(trig[i][:], 1.0)
 
         def g_inter(i):
-            c0 = PEW + s_cols(i)
+            c0 = pe_cols(i)
             nc.gpsimd.tensor_scalar(
                 out=grp[i][:, c0 : c0 + g_cols(i), :].rearrange("p (c q) t -> p c t q", q=8),
                 in0=wide[i][:, :, c0 : c0 + g_cols(i)].rearrange("p t (c q) -> p c t q", q=8),

@@ -70,8 +70,8 @@ def tile_multiheadattentionusingsdp_pa_kernel(
     with ExitStack() as ctx:
         const = ctx.enter_context(tc.tile_pool(name="const", bufs=1))
         wbp = ctx.enter_context(tc.tile_pool(name="wbp", bufs=AHEAD + 8))
-        widep = ctx.enter_context(tc.tile_pool(name="widep", bufs=LEAD + 3))
-        grpp = ctx.enter_context(tc.tile_pool(name="grpp", bufs=5))
+        widep = ctx.enter_context(tc.tile_pool(name="widep", bufs=LEAD + 5))
+        grpp = ctx.enter_context(tc.tile_pool(name="grpp", bufs=6))
         codep = ctx.enter_context(tc.tile_pool(name="codep", bufs=3))
         rotp = ctx.enter_context(tc.tile_pool(name="rotp", bufs=3))
         stp = ctx.enter_context(tc.tile_pool(name="stp", bufs=6))
@@ -124,9 +124,12 @@ def tile_multiheadattentionusingsdp_pa_kernel(
 
         for i in range(5):
             load(i)
-        craw = const.tile([P, 2, 2, 64], BF16, name="craw")
-        nc.sync.dma_start(out=craw[:, 0], in_=rope_cos.rearrange("(m p) d -> p m d", p=P))
-        nc.sync.dma_start(out=craw[:, 1], in_=rope_sin.rearrange("(m p) d -> p m d", p=P))
+        craw = const.tile([P, 2, 2, 2, 64], BF16, name="craw")
+        for c, table in ((0, rope_cos), (1, rope_sin)):
+            for half in range(2):
+                nc.sync.dma_start(
+                    out=craw[:, c, :, half, :], in_=table.rearrange("(m p) d -> p m d", p=P)
+                )
         nc.sync.dma_start(out=braw[0:32, :], in_=b_qkv[0 : 2 * D].rearrange("(c d) -> c d", d=HD))
         x_sb = const.tile([P, 2, D], BF16, name="x_sb")
         x_view = x.rearrange("o (m p) k -> p (o m) k", p=P)
@@ -137,8 +140,6 @@ def tile_multiheadattentionusingsdp_pa_kernel(
             load(i)
         bv = const.tile([P, D], BF16, name="bv")
 
-        zt = const.tile([P, 2, 2, P], F32, name="zt")
-        bf32 = const.tile([P, P], F32, name="bf32")
         cs = const.tile([P, 2, S_LEN], F32, name="cs")
         bias = const.tile([P, 32], F32, name="bias")
         xg = const.tile([P, PASSES, S_LEN, 4], BF16, name="xg", align_bytes=64)
@@ -159,17 +160,15 @@ def tile_multiheadattentionusingsdp_pa_kernel(
                     )
 
         def small_prep():
-            nc.vector.tensor_copy(out=zt[:, :, :, 0:64], in_=craw[:])
-            nc.vector.tensor_copy(out=zt[:, :, :, 64:128], in_=craw[:])
-            nc.vector.tensor_copy(out=bf32[:], in_=braw[:])
-            small["pcs"] = pso.tile([P, 2, S_LEN], F32, name="pcs", tag="o2")
+            small["pcs"] = pso.tile([P, 2, S_LEN], BF16, name="pcs", tag="o2")
             for c in range(2):
                 for m in range(2):
                     nc.tensor.transpose(
-                        small["pcs"][:, c, m * P : (m + 1) * P], zt[:, c, m, :], ident[:]
+                        small["pcs"][:, c, m * P : (m + 1) * P],
+                        craw[:, c, m].rearrange("p h d -> p (h d)"), identb[:],
                     )
-            small["pb"] = pso.tile([P, P], F32, name="pb", tag="o2")
-            nc.tensor.transpose(small["pb"][:], bf32[:], ident[:])
+            small["pb"] = pso.tile([P, P], BF16, name="pb", tag="o2")
+            nc.tensor.transpose(small["pb"][:], braw[:], identb[:])
 
         def small_out():
             nc.scalar.copy(out=cs[:, 0, :], in_=small["pcs"][:, 0, :])
@@ -182,10 +181,11 @@ def tile_multiheadattentionusingsdp_pa_kernel(
             nc.scalar.copy(out=xg[:, g].bitcast(F32), in_=xt[g][:].rearrange("p u r -> p r u"))
 
         def xquant(g):
+            two = slice(g, g + 2)
             nc.vector.quantize_mx(
-                out=xc[:, g, :].bitcast(FP8X4),
-                scales=xs[:, g, :],
-                in_=xg[:, g].rearrange("p r j -> p (r j)"),
+                out=xc[:, two, :].rearrange("p g r -> p (g r)").bitcast(FP8X4),
+                scales=xs[:, two, :].rearrange("p g r -> p (g r)"),
+                in_=xg[:, two].rearrange("p g r j -> p (g r j)"),
             )
 
         def plane(i, t):
@@ -322,8 +322,8 @@ def tile_multiheadattentionusingsdp_pa_kernel(
                     stop=(g == PASSES - 1),
                 )
 
-        def v_out(j):
-            for m in range(2):
+        def v_out(j, tokens=(0, 1)):
+            for m in tokens:
                 c0 = (j - ROT_CHUNKS) * NC
                 st = stp.tile([P, 4, HD], F32, name="st", tag="st")
                 nc.vector.tensor_tensor(
@@ -374,7 +374,6 @@ def tile_multiheadattentionusingsdp_pa_kernel(
                 x_transposes(3)
             if i in (4, 5):
                 xquant(2 * i - 8)
-                xquant(2 * i - 7)
             if pair_at(i - LAG) is not None:
                 mx_rot(pair_at(i - LAG))
             if 0 <= i + 2 < UNITS and g_cols(i + 2):
@@ -387,6 +386,8 @@ def tile_multiheadattentionusingsdp_pa_kernel(
             if i == (CHUNKS - 2) * PASSES:
                 v_out(CHUNKS - 4)
                 v_out(CHUNKS - 3)
+            if i == UNITS - 2:
+                v_out(CHUNKS - 2, (0,))
             if i == UNITS - 1:
-                v_out(CHUNKS - 2)
+                v_out(CHUNKS - 2, (1,))
                 v_out(CHUNKS - 1)

@@ -367,11 +367,8 @@ def tile_multiheadattentionusingsdp_pa_kernel(
                 quant(i)
             if i == 0:
                 small_prep()
-            if i == 1:
-                for p in range(3):
-                    x_transposes(p)
-            if i == 3:
-                x_transposes(3)
+            if 0 <= i < PASSES:
+                x_transposes(i)
             if i in (4, 5):
                 xquant(2 * i - 8)
             if pair_at(i - LAG) is not None:

from contextlib import ExitStack

import concourse.masks as masks
import concourse.mybir as mybir

F32 = mybir.dt.float32
BF16 = mybir.dt.bfloat16
U32 = mybir.dt.uint32
U8 = mybir.dt.uint8
FP8 = mybir.dt.float8_e4m3fn
FP8X4 = mybir.dt.float8_e4m3fn_x4
ACT = mybir.ActivationFunctionType
ALU = mybir.AluOpType

P = 128
S_LEN = 256
D = 2048
HD = 128
N_OUT = 3 * D
PASSES = 4
NC = 512
CHUNKS = N_OUT // NC
ROT_CHUNKS = 2 * D // NC
UNITS = CHUNKS * PASSES
PAIRS = 2 * ROT_CHUNKS
AHEAD = 16
LEAD = 4
LAG = 5
PEW = 96
PEW_G = 128
SPLIT = 1
V_HEAD2 = 8
V_HEAD1 = 8
V_TAKE = (0, 1, 2)
V_STOP = 44
V_ALSO = 3
GW = 384
S_TAIL = 128

FLOPS = 2 * S_LEN * D * N_OUT


def v_planes(i):
    if i < V_HEAD2:
        return 2
    if i < V_HEAD1:
        return 1
    return 1 if ((i % 4 in V_TAKE or i % 4 == V_ALSO) and i < V_STOP) else 0


def s_cols(i):
    return S_TAIL if i == UNITS - 1 else 0


def g_cols(i):
    return GW if (i % 4 == 2 and 10 <= i <= 42) else 0


def pe_cols(i):
    return PEW_G if g_cols(i) else PEW


def tile_multiheadattentionusingsdp_pa_kernel(
    tc, x, w_qkv_bytes, w_qkv_scale, b_qkv, rope_cos, rope_sin, out_0, out_1, out_2
):
    nc = tc.nc
    outs = (out_0, out_1, out_2)
    w_view = w_qkv_bytes.rearrange("(g p t) n -> g p t n", g=PASSES, p=P, t=4)

    with ExitStack() as ctx:
        const = ctx.enter_context(tc.tile_pool(name="const", bufs=1))
        wbp = ctx.enter_context(tc.tile_pool(name="wbp", bufs=AHEAD + 8))
        widep = ctx.enter_context(tc.tile_pool(name="widep", bufs=LEAD + 5))
        grpp = ctx.enter_context(tc.tile_pool(name="grpp", bufs=6))
        codep = ctx.enter_context(tc.tile_pool(name="codep", bufs=3))
        rotp = ctx.enter_context(tc.tile_pool(name="rotp", bufs=3))
        stp = ctx.enter_context(tc.tile_pool(name="stp", bufs=6))
        trigp = ctx.enter_context(tc.tile_pool(name="trigp", bufs=2))
        psa = ctx.enter_context(tc.psum_pool(name="psa", bufs=4))
        pso = ctx.enter_context(tc.psum_pool(name="pso", bufs=2))
        psi = ctx.enter_context(tc.psum_pool(name="psi", bufs=2))
        ctx.enter_context(tc.manual_schedule())

        wb = {}
        wide = {}
        grp = {}
        pint = {}
        wc = {}
        ws = {}
        acc = {}
        rot = {}
        o2 = {}
        trig = {}

        def load(i):
            j, g = divmod(i, PASSES)
            wb[i] = wbp.tile([P, 4, NC], U8, name="wb", tag="wb")
            src = w_view[g][:, :, j * NC : (j + 1) * NC]
            if i < SPLIT:
                for t in (0, 2):
                    nc.sync.dma_start(out=wb[i][:, t : t + 2, :], in_=src[:, t : t + 2, :])
            else:
                nc.sync.dma_start(out=wb[i][:], in_=src)

        warm = const.tile([P, 2], F32, name="warm")
        nc.vector.memset(warm[:], 0.0)
        sc = const.tile([P, PASSES, 4], F32, name="sc")
        nc.scalar.dma_start(
            out=sc[:], in_=w_qkv_scale.rearrange("(g p t) o -> p g (t o)", g=PASSES, p=P, t=4)
        )
        nc.scalar.activation(out=warm[:, 1:2], in_=warm[:, 0:1], func=ACT.Copy)
        sgn = const.tile([P, 1], F32, name="sgn")
        nc.vector.memset(sgn[0:64, :], 1.0)
        nc.vector.memset(sgn[64:128, :], -1.0)
        ident = const.tile([P, P], F32, name="ident")
        masks.make_identity(nc, ident[:])
        braw = const.tile([P, P], BF16, name="braw")
        nc.gpsimd.memset(braw[:], 0.0)
        identb = const.tile([P, P], BF16, name="identb")
        nc.vector.tensor_copy(out=identb[:], in_=ident[:])
        perm = const.tile([P, P], F32, name="perm")
        nc.vector.tensor_copy(out=perm[:, 0:64], in_=ident[:, 64:128])
        nc.vector.tensor_copy(out=perm[:, 64:128], in_=ident[:, 0:64])

        for i in range(5):
            load(i)
        craw = const.tile([P, 2, 2, 2, 64], BF16, name="craw")
        for c, table in ((0, rope_cos), (1, rope_sin)):
            for half in range(2):
                nc.sync.dma_start(
                    out=craw[:, c, :, half, :], in_=table.rearrange("(m p) d -> p m d", p=P)
                )
        nc.sync.dma_start(out=braw[0:32, :], in_=b_qkv[0 : 2 * D].rearrange("(c d) -> c d", d=HD))
        x_sb = const.tile([P, 2, D], BF16, name="x_sb")
        x_view = x.rearrange("o (m p) k -> p (o m) k", p=P)
        nc.sync.dma_start(out=x_sb[:, 0, :], in_=x_view[:, 0, :])
        load(5)
        nc.sync.dma_start(out=x_sb[:, 1, :], in_=x_view[:, 1, :])
        for i in range(6, AHEAD - LEAD):
            load(i)
        bv = const.tile([P, D], BF16, name="bv")

        cs = const.tile([P, 2, S_LEN], F32, name="cs")
        bias = const.tile([P, 32], F32, name="bias")
        xg = const.tile([P, PASSES, S_LEN, 4], BF16, name="xg", align_bytes=64)
        xc = const.tile([P, PASSES, S_LEN], U32, name="xc", align_bytes=64)
        xs = const.tile([P, PASSES, S_LEN], U8, name="xs", align_bytes=64)
        xt = {}
        small = {}

        def x_transposes(g):
            xt[g] = psa.tile([P, 2, S_LEN], F32, name="xt", tag="acc")
            for m in range(2):
                words = x_sb[:, m, :].bitcast(F32)
                for u in range(2):
                    nc.tensor.transpose(
                        xt[g][:, u, m * P : (m + 1) * P],
                        words[:, 256 * g + u : 256 * (g + 1) : 2],
                        ident[:],
                    )

        def small_prep():
            small["pcs"] = pso.tile([P, 2, S_LEN], BF16, name="pcs", tag="o2")
            for c in range(2):
                for m in range(2):
                    nc.tensor.transpose(
                        small["pcs"][:, c, m * P : (m + 1) * P],
                        craw[:, c, m].rearrange("p h d -> p (h d)"), identb[:],
                    )
            small["pb"] = pso.tile([P, P], BF16, name="pb", tag="o2")
            nc.tensor.transpose(small["pb"][:], braw[:], identb[:])

        def small_out():
            nc.scalar.copy(out=cs[:, 0, :], in_=small["pcs"][:, 0, :])
            nc.scalar.activation(
                out=cs[:, 1, :], in_=small["pcs"][:, 1, :], func=ACT.Copy, scale=sgn[:, 0:1]
            )
            nc.scalar.copy(out=bias[:], in_=small["pb"][:, 0:32])

        def xcopy(g):
            nc.scalar.copy(out=xg[:, g].bitcast(F32), in_=xt[g][:].rearrange("p u r -> p r u"))

        def xquant(g):
            two = slice(g, g + 2)
            nc.vector.quantize_mx(
                out=xc[:, two, :].rearrange("p g r -> p (g r)").bitcast(FP8X4),
                scales=xs[:, two, :].rearrange("p g r -> p (g r)"),
                in_=xg[:, two].rearrange("p g r j -> p (g r j)"),
            )

        def plane(i, t):
            g = i % PASSES
            if t == 0:
                wide[i] = widep.tile([P, 4, NC], BF16, name="wide", tag="wide")
            src = wb[i][:, t, :].bitcast(FP8)
            if t >= 4 - v_planes(i):
                nc.vector.tensor_scalar(
                    out=wide[i][:, t, :], in0=src, scalar1=sc[:, g, t : t + 1],
                    scalar2=None, op0=ALU.mult,
                )
            else:
                nc.scalar.activation(
                    out=wide[i][:, t, :], in_=src, func=ACT.Copy, scale=sc[:, g, t : t + 1]
                )

        def pe_inter(i):
            pint[i] = psi.tile([P, pe_cols(i), 4], BF16, name="pint", tag="pint")
            nc.tensor.matmul(
                out=pint[i][:].rearrange("p n t -> p (n t)"),
                lhsT=identb[:],
                rhs=wide[i][:, :, 0 : pe_cols(i)].rearrange("p t n -> p n t"),
                start=True, stop=True,
            )

        def pe_evac(i):
            grp[i] = grpp.tile([P, NC, 4], BF16, name="grp", tag="grp", align_bytes=64)
            nc.scalar.copy(out=grp[i][:, 0 : pe_cols(i), :], in_=pint[i][:])
            sw = s_cols(i)
            if sw:
                nc.scalar.copy(
                    out=grp[i][:, PEW : PEW + sw, :],
                    in_=wide[i][:, :, PEW : PEW + sw].rearrange("p t n -> p n t"),
                )

        def inter(i):
            c0 = pe_cols(i) + s_cols(i) + g_cols(i)
            if c0 == NC:
                return
            nc.vector.tensor_copy(
                out=grp[i][:, c0:NC, :].rearrange("p (c q) t -> p c t q", q=8),
                in_=wide[i][:, :, c0:NC].rearrange("p t (c q) -> p c t q", q=8),
            )

        def g_trig(i):
            trig[i] = trigp.tile([P, 1], F32, name="trig", tag="trig")
            nc.vector.memset(trig[i][:], 1.0)

        def g_inter(i):
            c0 = pe_cols(i)
            nc.gpsimd.tensor_scalar(
                out=grp[i][:, c0 : c0 + g_cols(i), :].rearrange("p (c q) t -> p c t q", q=8),
                in0=wide[i][:, :, c0 : c0 + g_cols(i)].rearrange("p t (c q) -> p c t q", q=8),
                scalar1=trig[i][:, 0:1], scalar2=0.0, op0=ALU.mult, op1=ALU.add,
            )

        def quant(i):
            j, g = divmod(i, PASSES)
            if g == 0:
                wc[j] = codep.tile([P, PASSES, NC], U32, name="wc", tag="wc", align_bytes=64)
                ws[j] = codep.tile([P, PASSES, NC], U8, name="ws", tag="ws", align_bytes=64)
            nc.vector.quantize_mx(
                out=wc[j][:, g, :].bitcast(FP8X4),
                scales=ws[j][:, g, :],
                in_=grp[i][:].rearrange("p n t -> p (n t)"),
            )

        def mx_rot(q):
            j, pr = divmod(q, 2)
            acc[q] = psa.tile([P, 2, S_LEN], F32, name="acc", tag="acc")
            for e in range(2):
                cols = slice((2 * pr + e) * HD, (2 * pr + e + 1) * HD)
                for g in range(PASSES):
                    nc.tensor.matmul_mx(
                        out=acc[q][:, e, :],
                        lhsT=wc[j][:, g, cols].bitcast(FP8X4),
                        lhsT_scale=ws[j][:, g, cols],
                        rhs=xc[:, g, :].bitcast(FP8X4),
                        rhs_scale=xs[:, g, :],
                        start=(g == 0),
                        stop=(g == PASSES - 1),
                    )

        def rope(q):
            r = rotp.tile([P, 2, 2, S_LEN], F32, name="rot", tag="rot")
            for e in range(2):
                c = 2 * q + e
                nc.vector.scalar_tensor_tensor(
                    out=r[:, :, e, :],
                    in0=acc[q][:, e, :].unsqueeze(1).to_broadcast([P, 2, S_LEN]),
                    scalar=bias[:, c : c + 1],
                    in1=cs[:], op0=ALU.add, op1=ALU.mult,
                )
            o2[q] = pso.tile([P, 2, 2, HD], F32, name="o2", tag="o2")
            for e in range(2):
                for m in range(2):
                    tok = slice(m * P, (m + 1) * P)
                    nc.tensor.matmul(
                        out=o2[q][:, m, e, :], lhsT=r[:, 0, e, tok], rhs=ident[:],
                        is_transpose=True, start=True, stop=False,
                    )
                    nc.tensor.matmul(
                        out=o2[q][:, m, e, :], lhsT=r[:, 1, e, tok], rhs=perm[:],
                        is_transpose=True, start=False, stop=True,
                    )

        def evac(q):
            st = stp.tile([P, 2, 2, HD], F32, name="st", tag="st")
            nc.scalar.copy(out=st[:], in_=o2[q][:])
            dst = outs[q // 8]
            h0 = 2 * (q % 8)
            for m in range(2):
                nc.sync.dma_start(
                    out=dst[0, h0 : h0 + 2, m * P : (m + 1) * P, :].rearrange("h s d -> s h d"),
                    in_=st[:, m],
                )

        def mx_v(i):
            j, g = divmod(i, PASSES)
            for m in range(2):
                if g == 0 and j != CHUNKS - 2:
                    acc[(j, m)] = psa.tile([P, NC], F32, name="accv", tag="acc")
                elif g == 0:
                    acc[(j, m)] = pso.tile([P, NC], F32, name="accv", tag="o2")
                tok = slice(m * P, (m + 1) * P)
                nc.tensor.matmul_mx(
                    out=acc[(j, m)][:],
                    lhsT=xc[:, g, tok].bitcast(FP8X4),
                    lhsT_scale=xs[:, g, tok],
                    rhs=wc[j][:, g, :].bitcast(FP8X4),
                    rhs_scale=ws[j][:, g, :],
                    start=(g == 0),
                    stop=(g == PASSES - 1),
                )

        def v_out(j, tokens=(0, 1)):
            for m in tokens:
                c0 = (j - ROT_CHUNKS) * NC
                st = stp.tile([P, 4, HD], F32, name="st", tag="st")
                nc.vector.tensor_tensor(
                    out=st[:].rearrange("p h d -> p (h d)"), in0=acc[(j, m)][:],
                    in1=bv[:, c0 : c0 + NC], op=ALU.add,
                )
                h0 = c0 // HD
                nc.sync.dma_start(
                    out=out_2[0, h0 : h0 + 4, m * P : (m + 1) * P, :].rearrange("h s d -> s h d"),
                    in_=st[:],
                )

        def pair_at(step):
            j, r = divmod(step, PASSES)
            return 2 * j + r if (r < 2 and 0 <= j < ROT_CHUNKS) else None

        for i in range(-LEAD, UNITS + LAG + 6):
            j, g = divmod(i, PASSES)
            if 0 <= i + AHEAD < UNITS:
                load(i + AHEAD)
            if i == 8:
                nc.sync.dma_start(out=bv[:], in_=b_qkv[2 * D : 3 * D].partition_broadcast(P))
            if i == 2:
                small_out()
            if 0 <= i - 2 < PASSES:
                xcopy(i - 2)
            for t in range(4):
                if 0 <= i + LEAD < UNITS:
                    plane(i + LEAD, t)
                if t == 1 and 0 <= i + 2 < UNITS:
                    pe_evac(i + 2)
                if t == 2 and pair_at(i - LAG - 5) is not None:
                    evac(pair_at(i - LAG - 5))
            if 0 <= i + LEAD < UNITS:
                pe_inter(i + LEAD)
            if 0 <= i + 1 < UNITS:
                inter(i + 1)
            if 0 <= i + 2 < UNITS and g_cols(i + 2):
                g_trig(i + 2)
            if 0 <= i < UNITS:
                quant(i)
            if i == 0:
                small_prep()
            if 0 <= i < PASSES:
                x_transposes(i)
            if i in (4, 5):
                xquant(2 * i - 8)
            if pair_at(i - LAG) is not None:
                mx_rot(pair_at(i - LAG))
            if 0 <= i + 2 < UNITS and g_cols(i + 2):
                g_inter(i + 2)
            if pair_at(i - LAG - 2) is not None and pair_at(i - LAG - 2) % 2 == 1:
                rope(pair_at(i - LAG - 2) - 1)
                rope(pair_at(i - LAG - 2))
            if ROT_CHUNKS * PASSES <= i < UNITS:
                mx_v(i)
            if i == (CHUNKS - 2) * PASSES:
                v_out(CHUNKS - 4)
                v_out(CHUNKS - 3)
            if i == UNITS - 2:
                v_out(CHUNKS - 2, (0,))
            if i == UNITS - 1:
                v_out(CHUNKS - 2, (1,))
                v_out(CHUNKS - 1)
